import numpy as np
import ml_dtypes


def mxq(x, axis, fmt="e4m3"):
    dtype, down = {"e4m3": (ml_dtypes.float8_e4m3fn, 7), "e5m2": (ml_dtypes.float8_e5m2, 14)}[fmt]
    v = np.moveaxis(np.asarray(x, np.float32).astype(ml_dtypes.bfloat16).astype(np.float64), axis, -1)
    blocks = v.reshape(v.shape[:-1] + (-1, 32))
    amax = np.abs(blocks).max(-1, keepdims=True)
    byte = np.maximum(np.where(amax > 0, np.frexp(amax)[1] - 1 + 127, 0) - down, 1)
    scale = np.exp2(byte - 127.0)
    codes = (blocks / scale).astype(np.float32).astype(dtype).astype(np.float64)
    return np.moveaxis((codes * scale).reshape(v.shape), -1, axis)


WIDE = False


def mx_kscale(k):
    if not WIDE:
        return np.ones(k)
    levels = np.array([10, -10, 5, -5, 0])
    a = np.random.permutation(np.resize(levels, k // 512 * 4)).reshape(k // 512, 4)
    idx = np.arange(k)
    return np.exp2(a[idx // 512, idx % 128 // 32])


BF16 = ml_dtypes.bfloat16


def bf(x):
    return np.asarray(x, np.float32).astype(BF16)


def f64(x):
    return np.asarray(x).astype(np.float64)


B, CQ, CR, HID, H, W = 16, 1024, 512, 512, 16, 16
P = H * W


def setup_inputs():
    s, r, t = mx_kscale(CQ), mx_kscale(CR), mx_kscale(HID)
    return {"query_features": bf(np.random.standard_normal((B, CQ, H, W)) * s[None, :, None, None]),
            "reference_features": bf(np.random.standard_normal((B, CR, H, W)) * r[None, :, None, None]),
            "Wq": bf(np.random.standard_normal((HID, CQ)) * 0.4 / np.sqrt(CQ) * t[:, None] / s[None, :]),
            "bq": bf(np.random.standard_normal(HID) * 0.1 * t),
            "Wk": bf(np.random.standard_normal((HID, CR)) * 0.4 / np.sqrt(CR) / t[:, None] / r[None, :]),
            "bk": bf(np.random.standard_normal(HID) * 0.1 / t)}


def reference(query_features, reference_features, Wq, bq, Wk, bk):
    xq = f64(query_features).reshape(B, CQ, P)
    xr = f64(reference_features).reshape(B, CR, P)
    Q = (mxq(f64(Wq), 1, "e4m3") @ mxq(xq, 1, "e4m3")) + f64(bq)[None, :, None]
    K = (mxq(f64(Wk), 1, "e4m3") @ mxq(xr, 1, "e4m3")) + f64(bk)[None, :, None]
    attn = mxq(Q, 1, "e4m3").transpose(0, 2, 1) @ mxq(K, 1, "e4m3")
    return attn.reshape(B, H, W, P)

@@ -1,0 +1,190 @@
+import concourse.mybir as mybir
+from concourse.masks import make_identity
+
+F32 = mybir.dt.float32
+BF16 = mybir.dt.bfloat16
+U32 = mybir.dt.uint32
+U8 = mybir.dt.uint8
+FP8X4 = mybir.dt.float8_e4m3fn_x4
+ADD = mybir.AluOpType.add
+
+P = 128
+PACK = 4
+K_PASS = P * PACK
+BANK = 512
+
+IMAGES = 16
+PIX = 256
+HALVES = PIX // P
+CQ = 1024
+CR = 512
+HID = 512
+Q_PASSES = CQ // K_PASS
+K_PASSES = CR // K_PASS
+
+VECTOR_REGROUP_IMAGES = 1
+
+FLOPS = 2 * IMAGES * PIX * (HID * CQ + HID * CR + PIX * HID)
+
+
+def quantise_weight(nc, stage, banks, ident, w, passes, codes, scales):
+    cols = passes * K_PASS
+    raw = stage.tile([P, PACK * cols], BF16, name="raw_w%d" % passes)
+    w_rows = w.rearrange("(m t) c -> m t c", t=PACK)
+    for t in range(PACK):
+        nc.sync.dma_start(out=raw[:, t * cols : (t + 1) * cols], in_=w_rows[:, t, :])
+    words = raw[:].bitcast(F32).rearrange(
+        "m (t g p u) -> m t g p u", t=PACK, g=passes, p=P, u=2
+    )
+    grouped = stage.tile([P, PACK * cols], BF16, name="grouped_w%d" % passes, align_bytes=64)
+    grouped_words = grouped[:].bitcast(F32).rearrange(
+        "p (g t m u) -> p g t m u", g=passes, t=PACK, m=P, u=2
+    )
+    for t in range(PACK):
+        bank = banks.tile([P, BANK], F32, tag="bank")
+        for g in range(passes):
+            for u in range(2):
+                first = (g * 2 + u) * P
+                nc.tensor.transpose(bank[:, first : first + P], words[:, t, g, :, u], ident[:])
+        nc.scalar.copy(
+            out=grouped_words[:, :, t, :, :],
+            in_=bank[:, : passes * 2 * P].rearrange("p (g u m) -> p g m u", g=passes, u=2),
+        )
+    nc.vector.quantize_mx(out=codes.bitcast(FP8X4), scales=scales, in_=grouped[:])
+
+
+def regroup(copy, grouped, raw):
+    copy(
+        out=grouped.rearrange("p (c i j) -> p c j i", i=4, j=PACK),
+        in_=raw.rearrange("p (j c i) -> p c j i", j=PACK, i=4),
+    )
+
+
+def project(nc, banks, work, keep, x_codes, x_scales, w_codes, w_scales, passes, bias, name):
+    grouped = work.tile([P, PIX, PACK], BF16, name="grouped_" + name, align_bytes=64)
+    for half in range(HALVES):
+        bank = banks.tile([P, BANK], F32, tag="bank")
+        for t in range(PACK):
+            for g in range(passes):
+                w_cols = slice((g * PACK + t) * P, (g * PACK + t + 1) * P)
+                x_cols = slice(g * PIX + half * P, g * PIX + (half + 1) * P)
+                nc.tensor.matmul_mx(
+                    out=bank[:, t * P : (t + 1) * P],
+                    lhsT=w_codes[:, w_cols].bitcast(FP8X4),
+                    lhsT_scale=w_scales[:, w_cols],
+                    rhs=x_codes[:, x_cols].bitcast(FP8X4),
+                    rhs_scale=x_scales[:, x_cols],
+                    start=(g == 0),
+                    stop=(g == passes - 1),
+                )
+        nc.vector.tensor_tensor(
+            out=grouped[:, half * P : (half + 1) * P, :],
+            in0=bank[:].rearrange("p (t w) -> p w t", t=PACK),
+            in1=bias.unsqueeze(1).to_broadcast([P, P, PACK]),
+            op=ADD,
+        )
+    codes = keep.tile([P, PIX], U32, name="codes_" + name, align_bytes=64)
+    scales = keep.tile([P, PIX], U8, name="scales_" + name, align_bytes=64)
+    nc.vector.quantize_mx(
+        out=codes[:].bitcast(FP8X4),
+        scales=scales[:],
+        in_=grouped[:].rearrange("p w t -> p (w t)"),
+    )
+    return codes, scales
+
+
+def tile_crossattentionvaluefuser_pa_t_kernel(
+    tc, query_features, reference_features, Wq, bq, Wk, bk, out
+):
+    nc = tc.nc
+    xq_dram = query_features.rearrange("b (g p j) h w -> b p g (j h w)", g=Q_PASSES, p=P, j=PACK)
+    xr_dram = reference_features.rearrange("b (p j) h w -> b p (j h w)", p=P, j=PACK)
+    out_dram = out.rearrange("b (a i) j n -> b (i j) a n", a=HALVES)
+
+    with tc.tile_pool(name="const", bufs=1) as const, tc.tile_pool(
+        name="stage", bufs=1
+    ) as stage, tc.tile_pool(name="inputs", bufs=IMAGES) as inputs, tc.tile_pool(
+        name="work", bufs=4
+    ) as work, tc.tile_pool(name="keep", bufs=4) as keep, tc.tile_pool(
+        name="results", bufs=6
+    ) as results, tc.psum_pool(name="banks", bufs=6) as banks, tc.psum_pool(
+        name="logits", bufs=2
+    ) as logits:
+        ident = const.tile([P, P], F32)
+        make_identity(nc, ident[:])
+
+        bq_raw = const.tile([P, PACK], BF16)
+        bk_raw = const.tile([P, PACK], BF16)
+        nc.scalar.dma_start(out=bk_raw[:], in_=bk.rearrange("(p t) -> p t", t=PACK))
+        nc.scalar.dma_start(out=bq_raw[:], in_=bq.rearrange("(p t) -> p t", t=PACK))
+        bq_f32 = const.tile([P, PACK], F32)
+        bk_f32 = const.tile([P, PACK], F32)
+        nc.vector.tensor_copy(out=bk_f32[:], in_=bk_raw[:])
+        nc.vector.tensor_copy(out=bq_f32[:], in_=bq_raw[:])
+
+        wk_codes = const.tile([P, K_PASSES * HID], U32, align_bytes=64)
+        wk_scales = const.tile([P, K_PASSES * HID], U8, align_bytes=64)
+        wq_codes = const.tile([P, Q_PASSES * HID], U32, align_bytes=64)
+        wq_scales = const.tile([P, Q_PASSES * HID], U8, align_bytes=64)
+
+        xr_raws = []
+        xq_raws = []
+        for b in range(IMAGES):
+            xr_raw = inputs.tile([P, PACK * PIX], BF16)
+            nc.sync.dma_start(out=xr_raw[:], in_=xr_dram[b])
+            xr_raws.append(xr_raw)
+            if b == 0:
+                quantise_weight(nc, stage, banks, ident, Wk, K_PASSES, wk_codes[:], wk_scales[:])
+            xq_raw = inputs.tile([P, Q_PASSES, PACK * PIX], BF16)
+            nc.sync.dma_start(out=xq_raw[:], in_=xq_dram[b])
+            xq_raws.append(xq_raw)
+            if b == 0:
+                quantise_weight(nc, stage, banks, ident, Wq, Q_PASSES, wq_codes[:], wq_scales[:])
+
+        for b in range(IMAGES):
+            copy = nc.vector.tensor_copy if b < VECTOR_REGROUP_IMAGES else nc.scalar.copy
+
+            xr_grouped = work.tile([P, PACK * PIX], BF16, align_bytes=64)
+            regroup(copy, xr_grouped[:], xr_raws[b][:])
+            xr_codes = keep.tile([P, PIX], U32, align_bytes=64)
+            xr_scales = keep.tile([P, PIX], U8, align_bytes=64)
+            nc.vector.quantize_mx(
+                out=xr_codes[:].bitcast(FP8X4), scales=xr_scales[:], in_=xr_grouped[:]
+            )
+
+            xq_grouped = work.tile([P, Q_PASSES * PACK * PIX], BF16, align_bytes=64)
+            for g in range(Q_PASSES):
+                regroup(
+                    copy,
+                    xq_grouped[:, g * PACK * PIX : (g + 1) * PACK * PIX],
+                    xq_raws[b][:, g, :],
+                )
+            xq_codes = keep.tile([P, Q_PASSES * PIX], U32, align_bytes=64)
+            xq_scales = keep.tile([P, Q_PASSES * PIX], U8, align_bytes=64)
+            nc.vector.quantize_mx(
+                out=xq_codes[:].bitcast(FP8X4), scales=xq_scales[:], in_=xq_grouped[:]
+            )
+
+            k_codes, k_scales = project(
+                nc, banks, work, keep, xr_codes, xr_scales, wk_codes, wk_scales,
+                K_PASSES, bk_f32[:], "k",
+            )
+            q_codes, q_scales = project(
+                nc, banks, work, keep, xq_codes, xq_scales, wq_codes, wq_scales,
+                Q_PASSES, bq_f32[:], "q",
+            )
+
+            logit = logits.tile([P, HALVES, PIX], F32)
+            for a in range(HALVES):
+                nc.tensor.matmul_mx(
+                    out=logit[:, a, :],
+                    lhsT=q_codes[:, a * P : (a + 1) * P].bitcast(FP8X4),
+                    lhsT_scale=q_scales[:, a * P : (a + 1) * P],
+                    rhs=k_codes[:].bitcast(FP8X4),
+                    rhs_scale=k_scales[:],
+                    start=True,
+                    stop=True,
+                )
+            result = results.tile([P, HALVES, PIX], F32)
+            nc.scalar.copy(out=result[:], in_=logit[:])
+            nc.sync.dma_start(out=out_dram[b], in_=result[:])

@@ -1,3 +1,5 @@
+from contextlib import ExitStack
+
 import concourse.mybir as mybir
 from concourse.masks import make_identity
 
@@ -16,175 +18,234 @@ BANK = 512
 IMAGES = 16
 PIX = 256
 HALVES = PIX // P
-CQ = 1024
-CR = 512
 HID = 512
-Q_PASSES = CQ // K_PASS
-K_PASSES = CR // K_PASS
 
-VECTOR_REGROUP_IMAGES = 1
+LEAD = 3
 
-FLOPS = 2 * IMAGES * PIX * (HID * CQ + HID * CR + PIX * HID)
-
-
-def quantise_weight(nc, stage, banks, ident, w, passes, codes, scales):
-    cols = passes * K_PASS
-    raw = stage.tile([P, PACK * cols], BF16, name="raw_w%d" % passes)
-    w_rows = w.rearrange("(m t) c -> m t c", t=PACK)
-    for t in range(PACK):
-        nc.sync.dma_start(out=raw[:, t * cols : (t + 1) * cols], in_=w_rows[:, t, :])
-    words = raw[:].bitcast(F32).rearrange(
-        "m (t g p u) -> m t g p u", t=PACK, g=passes, p=P, u=2
-    )
-    grouped = stage.tile([P, PACK * cols], BF16, name="grouped_w%d" % passes, align_bytes=64)
-    grouped_words = grouped[:].bitcast(F32).rearrange(
-        "p (g t m u) -> p g t m u", g=passes, t=PACK, m=P, u=2
-    )
-    for t in range(PACK):
-        bank = banks.tile([P, BANK], F32, tag="bank")
-        for g in range(passes):
-            for u in range(2):
-                first = (g * 2 + u) * P
-                nc.tensor.transpose(bank[:, first : first + P], words[:, t, g, :, u], ident[:])
-        nc.scalar.copy(
-            out=grouped_words[:, :, t, :, :],
-            in_=bank[:, : passes * 2 * P].rearrange("p (g u m) -> p g m u", g=passes, u=2),
-        )
-    nc.vector.quantize_mx(out=codes.bitcast(FP8X4), scales=scales, in_=grouped[:])
-
-
-def regroup(copy, grouped, raw):
-    copy(
-        out=grouped.rearrange("p (c i j) -> p c j i", i=4, j=PACK),
-        in_=raw.rearrange("p (j c i) -> p c j i", j=PACK, i=4),
-    )
-
-
-def project(nc, banks, work, keep, x_codes, x_scales, w_codes, w_scales, passes, bias, name):
-    grouped = work.tile([P, PIX, PACK], BF16, name="grouped_" + name, align_bytes=64)
-    for half in range(HALVES):
-        bank = banks.tile([P, BANK], F32, tag="bank")
-        for t in range(PACK):
-            for g in range(passes):
-                w_cols = slice((g * PACK + t) * P, (g * PACK + t + 1) * P)
-                x_cols = slice(g * PIX + half * P, g * PIX + (half + 1) * P)
-                nc.tensor.matmul_mx(
-                    out=bank[:, t * P : (t + 1) * P],
-                    lhsT=w_codes[:, w_cols].bitcast(FP8X4),
-                    lhsT_scale=w_scales[:, w_cols],
-                    rhs=x_codes[:, x_cols].bitcast(FP8X4),
-                    rhs_scale=x_scales[:, x_cols],
-                    start=(g == 0),
-                    stop=(g == passes - 1),
-                )
-        nc.vector.tensor_tensor(
-            out=grouped[:, half * P : (half + 1) * P, :],
-            in0=bank[:].rearrange("p (t w) -> p w t", t=PACK),
-            in1=bias.unsqueeze(1).to_broadcast([P, P, PACK]),
-            op=ADD,
-        )
-    codes = keep.tile([P, PIX], U32, name="codes_" + name, align_bytes=64)
-    scales = keep.tile([P, PIX], U8, name="scales_" + name, align_bytes=64)
-    nc.vector.quantize_mx(
-        out=codes[:].bitcast(FP8X4),
-        scales=scales[:],
-        in_=grouped[:].rearrange("p w t -> p (w t)"),
-    )
-    return codes, scales
+FLOPS = 2 * IMAGES * PIX * (HID * 1024 + HID * 512 + PIX * HID)
 
 
 def tile_crossattentionvaluefuser_pa_t_kernel(
     tc, query_features, reference_features, Wq, bq, Wk, bk, out
 ):
     nc = tc.nc
-    xq_dram = query_features.rearrange("b (g p j) h w -> b p g (j h w)", g=Q_PASSES, p=P, j=PACK)
-    xr_dram = reference_features.rearrange("b (p j) h w -> b p (j h w)", p=P, j=PACK)
+    k_side = {"name": "k", "x": reference_features, "w": Wk, "b": bk, "vector_images": LEAD}
+    q_side = {"name": "q", "x": query_features, "w": Wq, "b": bq, "vector_images": 1}
+    for side in (k_side, q_side):
+        side["passes"] = side["w"].shape[1] // K_PASS
     out_dram = out.rearrange("b (a i) j n -> b (i j) a n", a=HALVES)
+    tiles = {}
 
-    with tc.tile_pool(name="const", bufs=1) as const, tc.tile_pool(
-        name="stage", bufs=1
-    ) as stage, tc.tile_pool(name="inputs", bufs=IMAGES) as inputs, tc.tile_pool(
-        name="work", bufs=4
-    ) as work, tc.tile_pool(name="keep", bufs=4) as keep, tc.tile_pool(
-        name="results", bufs=6
-    ) as results, tc.psum_pool(name="banks", bufs=6) as banks, tc.psum_pool(
-        name="logits", bufs=2
-    ) as logits:
-        ident = const.tile([P, P], F32)
-        make_identity(nc, ident[:])
+    with ExitStack() as ctx:
+        const = ctx.enter_context(tc.tile_pool(name="const", bufs=1))
+        inputs = ctx.enter_context(tc.tile_pool(name="inputs", bufs=IMAGES))
+        work = ctx.enter_context(tc.tile_pool(name="work", bufs=2))
+        banks = ctx.enter_context(tc.psum_pool(name="banks", bufs=6))
+        logit_banks = ctx.enter_context(tc.psum_pool(name="logit_banks", bufs=2))
+        ctx.enter_context(tc.manual_schedule())
 
-        bq_raw = const.tile([P, PACK], BF16)
-        bk_raw = const.tile([P, PACK], BF16)
-        nc.scalar.dma_start(out=bk_raw[:], in_=bk.rearrange("(p t) -> p t", t=PACK))
-        nc.scalar.dma_start(out=bq_raw[:], in_=bq.rearrange("(p t) -> p t", t=PACK))
-        bq_f32 = const.tile([P, PACK], F32)
-        bk_f32 = const.tile([P, PACK], F32)
-        nc.vector.tensor_copy(out=bk_f32[:], in_=bk_raw[:])
-        nc.vector.tensor_copy(out=bq_f32[:], in_=bq_raw[:])
+        def in_range(b):
+            return 0 <= b < IMAGES
 
-        wk_codes = const.tile([P, K_PASSES * HID], U32, align_bytes=64)
-        wk_scales = const.tile([P, K_PASSES * HID], U8, align_bytes=64)
-        wq_codes = const.tile([P, Q_PASSES * HID], U32, align_bytes=64)
-        wq_scales = const.tile([P, Q_PASSES * HID], U8, align_bytes=64)
+        def load(side, b):
+            if not in_range(b):
+                return
+            raw = inputs.tile([P, side["passes"], PACK * PIX], BF16, name="raw_" + side["name"])
+            nc.sync.dma_start(
+                out=raw[:],
+                in_=side["x"][b].rearrange("(g p j) h w -> p g (j h w)", p=P, j=PACK),
+            )
+            tiles["raw", side["name"], b] = raw
 
-        xr_raws = []
-        xq_raws = []
-        for b in range(IMAGES):
-            xr_raw = inputs.tile([P, PACK * PIX], BF16)
-            nc.sync.dma_start(out=xr_raw[:], in_=xr_dram[b])
-            xr_raws.append(xr_raw)
-            if b == 0:
-                quantise_weight(nc, stage, banks, ident, Wk, K_PASSES, wk_codes[:], wk_scales[:])
-            xq_raw = inputs.tile([P, Q_PASSES, PACK * PIX], BF16)
-            nc.sync.dma_start(out=xq_raw[:], in_=xq_dram[b])
-            xq_raws.append(xq_raw)
-            if b == 0:
-                quantise_weight(nc, stage, banks, ident, Wq, Q_PASSES, wq_codes[:], wq_scales[:])
-
-        for b in range(IMAGES):
-            copy = nc.vector.tensor_copy if b < VECTOR_REGROUP_IMAGES else nc.scalar.copy
-
-            xr_grouped = work.tile([P, PACK * PIX], BF16, align_bytes=64)
-            regroup(copy, xr_grouped[:], xr_raws[b][:])
-            xr_codes = keep.tile([P, PIX], U32, align_bytes=64)
-            xr_scales = keep.tile([P, PIX], U8, align_bytes=64)
-            nc.vector.quantize_mx(
-                out=xr_codes[:].bitcast(FP8X4), scales=xr_scales[:], in_=xr_grouped[:]
+        def load_weight(side):
+            cols = side["passes"] * K_PASS
+            raw = const.tile([P, PACK * cols], BF16, name="w_raw_" + side["name"])
+            rows = side["w"].rearrange("(m t) c -> m t c", t=PACK)
+            for t in range(PACK):
+                nc.sync.dma_start(out=raw[:, t * cols : (t + 1) * cols], in_=rows[:, t, :])
+            side["w_raw"] = raw
+            side["w_grouped"] = const.tile(
+                [P, PACK * cols], BF16, name="w_grouped_" + side["name"], align_bytes=64
+            )
+            side["w_codes"] = const.tile(
+                [P, cols], U32, name="w_codes_" + side["name"], align_bytes=64
+            )
+            side["w_scales"] = const.tile(
+                [P, cols], U8, name="w_scales_" + side["name"], align_bytes=64
+            )
+            side["bias"] = const.tile([P, PACK], BF16, name="bias_" + side["name"])
+            nc.scalar.dma_start(
+                out=side["bias"][:], in_=side["b"].rearrange("(p t) -> p t", t=PACK)
             )
 
-            xq_grouped = work.tile([P, Q_PASSES * PACK * PIX], BF16, align_bytes=64)
-            for g in range(Q_PASSES):
-                regroup(
-                    copy,
-                    xq_grouped[:, g * PACK * PIX : (g + 1) * PACK * PIX],
-                    xq_raws[b][:, g, :],
+        def transpose_weight(side, t):
+            passes = side["passes"]
+            words = side["w_raw"][:].bitcast(F32).rearrange(
+                "m (t g p u) -> m t g p u", t=PACK, g=passes, p=P, u=2
+            )
+            grouped_words = side["w_grouped"][:].bitcast(F32).rearrange(
+                "p (t g m u) -> p t g m u", t=PACK, g=passes, m=P, u=2
+            )
+            bank = banks.tile([P, BANK], F32, name="bank")
+            for g in range(passes):
+                for u in range(2):
+                    first = (g * 2 + u) * P
+                    nc.tensor.transpose(bank[:, first : first + P], words[:, t, g, :, u], ident[:])
+            nc.scalar.copy(
+                out=grouped_words[:, t, :, :, :],
+                in_=bank[:, : passes * 2 * P].rearrange("p (g u m) -> p g m u", g=passes, u=2),
+            )
+
+        def quantise_weight(side, t):
+            width = side["passes"] * P
+            nc.vector.quantize_mx(
+                out=side["w_codes"][:, t * width : (t + 1) * width].bitcast(FP8X4),
+                scales=side["w_scales"][:, t * width : (t + 1) * width],
+                in_=side["w_grouped"][:, t * PACK * width : (t + 1) * PACK * width],
+            )
+
+        def regroup(side, b):
+            if not in_range(b):
+                return
+            copy = nc.vector.tensor_copy if b < side["vector_images"] else nc.scalar.copy
+            grouped = work.tile(
+                [P, side["passes"], PACK * PIX], BF16,
+                name="x_grouped_" + side["name"], bufs=4, align_bytes=64,
+            )
+            for g in range(side["passes"]):
+                copy(
+                    out=grouped[:, g, :].rearrange("p (c i j) -> p c j i", i=4, j=PACK),
+                    in_=tiles["raw", side["name"], b][:, g, :].rearrange(
+                        "p (j c i) -> p c j i", j=PACK, i=4
+                    ),
                 )
-            xq_codes = keep.tile([P, Q_PASSES * PIX], U32, align_bytes=64)
-            xq_scales = keep.tile([P, Q_PASSES * PIX], U8, align_bytes=64)
+            tiles["x_grouped", side["name"], b] = grouped
+
+        def quantise(kind, side, b, width, bufs):
+            codes = work.tile(
+                [P, width], U32, name=kind + "_codes_" + side["name"], bufs=bufs, align_bytes=64
+            )
+            scales = work.tile(
+                [P, width], U8, name=kind + "_scales_" + side["name"], bufs=bufs, align_bytes=64
+            )
             nc.vector.quantize_mx(
-                out=xq_codes[:].bitcast(FP8X4), scales=xq_scales[:], in_=xq_grouped[:]
+                out=codes[:].bitcast(FP8X4),
+                scales=scales[:],
+                in_=tiles[kind + "_grouped", side["name"], b][:].rearrange("p a b -> p (a b)"),
             )
+            tiles[kind + "_codes", side["name"], b] = codes
+            tiles[kind + "_scales", side["name"], b] = scales
 
-            k_codes, k_scales = project(
-                nc, banks, work, keep, xr_codes, xr_scales, wk_codes, wk_scales,
-                K_PASSES, bk_f32[:], "k",
-            )
-            q_codes, q_scales = project(
-                nc, banks, work, keep, xq_codes, xq_scales, wq_codes, wq_scales,
-                Q_PASSES, bq_f32[:], "q",
-            )
+        def quantise_x(side, b):
+            if in_range(b):
+                quantise("x", side, b, side["passes"] * PIX, 3)
 
-            logit = logits.tile([P, HALVES, PIX], F32)
+        def project(side, b):
+            if not in_range(b):
+                return
+            passes = side["passes"]
+            x_codes = tiles["x_codes", side["name"], b]
+            x_scales = tiles["x_scales", side["name"], b]
+            for half in range(HALVES):
+                bank = banks.tile([P, BANK], F32, name="bank")
+                for t in range(PACK):
+                    for g in range(passes):
+                        w_cols = slice((t * passes + g) * P, (t * passes + g + 1) * P)
+                        x_cols = slice(g * PIX + half * P, g * PIX + (half + 1) * P)
+                        nc.tensor.matmul_mx(
+                            out=bank[:, t * P : (t + 1) * P],
+                            lhsT=side["w_codes"][:, w_cols].bitcast(FP8X4),
+                            lhsT_scale=side["w_scales"][:, w_cols],
+                            rhs=x_codes[:, x_cols].bitcast(FP8X4),
+                            rhs_scale=x_scales[:, x_cols],
+                            start=(g == 0),
+                            stop=(g == passes - 1),
+                        )
+                tiles["bank", side["name"], b, half] = bank
+
+        def add_bias(side, b):
+            if not in_range(b):
+                return
+            grouped = work.tile(
+                [P, PIX, PACK], BF16, name="y_grouped_" + side["name"], align_bytes=64
+            )
+            for half in range(HALVES):
+                nc.vector.tensor_tensor(
+                    out=grouped[:, half * P : (half + 1) * P, :],
+                    in0=tiles["bank", side["name"], b, half][:].rearrange(
+                        "p (t w) -> p w t", t=PACK
+                    ),
+                    in1=side["bias"][:].unsqueeze(1).to_broadcast([P, P, PACK]),
+                    op=ADD,
+                )
+            tiles["y_grouped", side["name"], b] = grouped
+
+        def quantise_y(side, b, bufs):
+            if in_range(b):
+                quantise("y", side, b, PIX, bufs)
+
+        def logits(b):
+            if not in_range(b):
+                return
+            logit = logit_banks.tile([P, HALVES, PIX], F32, name="logit")
             for a in range(HALVES):
                 nc.tensor.matmul_mx(
                     out=logit[:, a, :],
-                    lhsT=q_codes[:, a * P : (a + 1) * P].bitcast(FP8X4),
-                    lhsT_scale=q_scales[:, a * P : (a + 1) * P],
-                    rhs=k_codes[:].bitcast(FP8X4),
-                    rhs_scale=k_scales[:],
+                    lhsT=tiles["y_codes", "q", b][:, a * P : (a + 1) * P].bitcast(FP8X4),
+                    lhsT_scale=tiles["y_scales", "q", b][:, a * P : (a + 1) * P],
+                    rhs=tiles["y_codes", "k", b][:].bitcast(FP8X4),
+                    rhs_scale=tiles["y_scales", "k", b][:],
                     start=True,
                     stop=True,
                 )
-            result = results.tile([P, HALVES, PIX], F32)
-            nc.scalar.copy(out=result[:], in_=logit[:])
+            tiles["logit", b] = logit
+
+        def store(b):
+            if not in_range(b):
+                return
+            result = work.tile([P, HALVES, PIX], F32, name="result", bufs=6)
+            nc.scalar.copy(out=result[:], in_=tiles["logit", b][:])
             nc.sync.dma_start(out=out_dram[b], in_=result[:])
+
+        ident = const.tile([P, P], F32, name="ident")
+        make_identity(nc, ident[:])
+
+        load(k_side, 0)
+        load_weight(k_side)
+        load(k_side, 1)
+        load_weight(q_side)
+        load(k_side, 2)
+        for b in range(IMAGES):
+            load(q_side, b)
+            load(k_side, b + LEAD)
+
+        regroup(k_side, 0)
+        quantise_x(k_side, 0)
+        for t in range(PACK):
+            transpose_weight(k_side, t)
+            quantise_weight(k_side, t)
+        regroup(k_side, 1)
+        quantise_x(k_side, 1)
+        regroup(k_side, 2)
+        project(k_side, 0)
+        for t in range(PACK):
+            transpose_weight(q_side, t)
+
+        for n in range(IMAGES + LEAD):
+            i = n - LEAD
+            add_bias(k_side, n)
+            project(k_side, n + 1)
+            add_bias(q_side, i)
+            if n == 1:
+                for t in range(PACK):
+                    quantise_weight(q_side, t)
+            project(q_side, i + 1)
+            store(i - 1)
+            regroup(k_side, n + 3)
+            regroup(q_side, i + 3)
+            quantise_x(k_side, n + 2)
+            quantise_x(q_side, i + 2)
+            quantise_y(k_side, n, LEAD + 2)
+            quantise_y(q_side, i, 2)
+            logits(i)
+        store(IMAGES - 1)

@@ -9,6 +9,7 @@ U32 = mybir.dt.uint32
 U8 = mybir.dt.uint8
 FP8X4 = mybir.dt.float8_e4m3fn_x4
 ADD = mybir.AluOpType.add
+MULT = mybir.AluOpType.mult
 
 P = 128
 PACK = 4
@@ -20,7 +21,8 @@ PIX = 256
 HALVES = PIX // P
 HID = 512
 
-LEAD = 3
+LEAD = 8
+AHEAD = 3
 
 FLOPS = 2 * IMAGES * PIX * (HID * 1024 + HID * 512 + PIX * HID)
 
@@ -29,12 +31,36 @@ def tile_crossattentionvaluefuser_pa_t_kernel(
     tc, query_features, reference_features, Wq, bq, Wk, bk, out
 ):
     nc = tc.nc
-    k_side = {"name": "k", "x": reference_features, "w": Wk, "b": bk, "vector_images": LEAD}
-    q_side = {"name": "q", "x": query_features, "w": Wq, "b": bq, "vector_images": 1}
+    sides = {
+        "k": {"name": "k", "x": reference_features, "w": Wk, "b": bk},
+        "q": {"name": "q", "x": query_features, "w": Wq, "b": bq},
+    }
+    k_side, q_side = sides["k"], sides["q"]
     for side in (k_side, q_side):
         side["passes"] = side["w"].shape[1] // K_PASS
     out_dram = out.rearrange("b (a i) j n -> b (i j) a n", a=HALVES)
     tiles = {}
+
+    steps = [(("k", b), ("k", b + 1)) for b in range(0, LEAD, 2)]
+    steps += [(("k", b + LEAD), ("q", b)) for b in range(IMAGES - LEAD)]
+    steps += [(("q", b), ("q", b + 1)) for b in range(IMAGES - LEAD, IMAGES, 2)]
+    where = {}
+    for s, pair in enumerate(steps):
+        for slot, job in enumerate(pair):
+            where[job] = (s, slot)
+
+    def units(s):
+        if not 0 <= s < len(steps):
+            return []
+        return [(n, b, g) for (n, b) in steps[s] for g in range(sides[n]["passes"])]
+
+    def engine_of(unit):
+        s = where[unit[:2]][0]
+        if s == 0:
+            return "vector"
+        if s >= 2 and unit == units(s)[-1]:
+            return "gpsimd"
+        return "scalar"
 
     with ExitStack() as ctx:
         const = ctx.enter_context(tc.tile_pool(name="const", bufs=1))
@@ -44,12 +70,7 @@ def tile_crossattentionvaluefuser_pa_t_kernel(
         logit_banks = ctx.enter_context(tc.psum_pool(name="logit_banks", bufs=2))
         ctx.enter_context(tc.manual_schedule())
 
-        def in_range(b):
-            return 0 <= b < IMAGES
-
         def load(side, b):
-            if not in_range(b):
-                return
             raw = inputs.tile([P, side["passes"], PACK * PIX], BF16, name="raw_" + side["name"])
             nc.sync.dma_start(
                 out=raw[:],
@@ -86,7 +107,10 @@ def tile_crossattentionvaluefuser_pa_t_kernel(
             grouped_words = side["w_grouped"][:].bitcast(F32).rearrange(
                 "p (t g m u) -> p t g m u", t=PACK, g=passes, m=P, u=2
             )
-            bank = banks.tile([P, BANK], F32, name="bank")
+            if side["name"] == "k":
+                bank = banks.tile([P, BANK], F32, name="bank")
+            else:
+                bank = logit_banks.tile([P, BANK], F32, name="logit")
             for g in range(passes):
                 for u in range(2):
                     first = (g * 2 + u) * P
@@ -104,148 +128,177 @@ def tile_crossattentionvaluefuser_pa_t_kernel(
                 in_=side["w_grouped"][:, t * PACK * width : (t + 1) * PACK * width],
             )
 
-        def regroup(side, b):
-            if not in_range(b):
-                return
-            copy = nc.vector.tensor_copy if b < side["vector_images"] else nc.scalar.copy
-            grouped = work.tile(
-                [P, side["passes"], PACK * PIX], BF16,
-                name="x_grouped_" + side["name"], bufs=4, align_bytes=64,
-            )
-            for g in range(side["passes"]):
-                copy(
-                    out=grouped[:, g, :].rearrange("p (c i j) -> p c j i", i=4, j=PACK),
-                    in_=tiles["raw", side["name"], b][:, g, :].rearrange(
-                        "p (j c i) -> p c j i", j=PACK, i=4
-                    ),
+        def regroup(unit):
+            name, b, g = unit
+            engine = engine_of(unit)
+            if engine == "scalar":
+                grouped = work.tile(
+                    [P, PACK * PIX], BF16, name="x_grouped", bufs=4 * (AHEAD + 1), align_bytes=64
                 )
-            tiles["x_grouped", side["name"], b] = grouped
+            else:
+                grouped = work.tile(
+                    [P, PACK * PIX], BF16, name="x_grouped_port", bufs=1, align_bytes=64
+                )
+            raw = tiles["raw", name, b]
+            if engine == "gpsimd":
+                nc.gpsimd.tensor_scalar(
+                    out=grouped[:].rearrange("p (w j) -> p w j", j=PACK),
+                    in0=raw[:, g, :].rearrange("p (j w) -> p w j", j=PACK),
+                    scalar1=1.0,
+                    scalar2=0.0,
+                    op0=MULT,
+                    op1=ADD,
+                )
+            else:
+                copy = nc.vector.tensor_copy if engine == "vector" else nc.scalar.copy
+                copy(
+                    out=grouped[:].rearrange("p (c i j) -> p c j i", i=4, j=PACK),
+                    in_=raw[:, g, :].rearrange("p (j c i) -> p c j i", j=PACK, i=4),
+                )
+            tiles["x_grouped", unit] = grouped
 
-        def quantise(kind, side, b, width, bufs):
-            codes = work.tile(
-                [P, width], U32, name=kind + "_codes_" + side["name"], bufs=bufs, align_bytes=64
+        def quantise_x(unit):
+            codes = work.tile([P, PIX], U32, name="x_codes", bufs=10, align_bytes=64)
+            scales = work.tile([P, PIX], U8, name="x_scales", bufs=10, align_bytes=64)
+            nc.vector.quantize_mx(
+                out=codes[:].bitcast(FP8X4), scales=scales[:], in_=tiles["x_grouped", unit][:]
             )
-            scales = work.tile(
-                [P, width], U8, name=kind + "_scales_" + side["name"], bufs=bufs, align_bytes=64
-            )
+            tiles["x_codes", unit] = codes
+            tiles["x_scales", unit] = scales
+
+        def project(s):
+            if not 0 <= s < len(steps):
+                return
+            for name, b in steps[s]:
+                side = sides[name]
+                passes = side["passes"]
+                for half in range(HALVES):
+                    bank = banks.tile([P, BANK], F32, name="bank")
+                    for t in range(PACK):
+                        for g in range(passes):
+                            w_cols = slice((t * passes + g) * P, (t * passes + g + 1) * P)
+                            x_cols = slice(half * P, (half + 1) * P)
+                            nc.tensor.matmul_mx(
+                                out=bank[:, t * P : (t + 1) * P],
+                                lhsT=side["w_codes"][:, w_cols].bitcast(FP8X4),
+                                lhsT_scale=side["w_scales"][:, w_cols],
+                                rhs=tiles["x_codes", (name, b, g)][:, x_cols].bitcast(FP8X4),
+                                rhs_scale=tiles["x_scales", (name, b, g)][:, x_cols],
+                                start=(g == 0),
+                                stop=(g == passes - 1),
+                            )
+                    tiles["bank", name, b, half] = bank
+
+        def add_bias(s):
+            grouped = work.tile([P, 2, PIX, PACK], BF16, name="y_grouped", bufs=2, align_bytes=64)
+            for slot, (name, b) in enumerate(steps[s]):
+                for half in range(HALVES):
+                    nc.vector.tensor_tensor(
+                        out=grouped[:, slot, half * P : (half + 1) * P, :],
+                        in0=tiles["bank", name, b, half][:].rearrange("p (t w) -> p w t", t=PACK),
+                        in1=sides[name]["bias"][:].unsqueeze(1).to_broadcast([P, P, PACK]),
+                        op=ADD,
+                    )
+            tiles["y_grouped", s] = grouped
+
+        def quantise_y(s):
+            codes = work.tile([P, 2 * PIX], U32, name="y_codes", bufs=LEAD + 2, align_bytes=64)
+            scales = work.tile([P, 2 * PIX], U8, name="y_scales", bufs=LEAD + 2, align_bytes=64)
             nc.vector.quantize_mx(
                 out=codes[:].bitcast(FP8X4),
                 scales=scales[:],
-                in_=tiles[kind + "_grouped", side["name"], b][:].rearrange("p a b -> p (a b)"),
+                in_=tiles["y_grouped", s][:].rearrange("p a w t -> p (a w t)"),
             )
-            tiles[kind + "_codes", side["name"], b] = codes
-            tiles[kind + "_scales", side["name"], b] = scales
+            tiles["y_codes", s] = codes
+            tiles["y_scales", s] = scales
 
-        def quantise_x(side, b):
-            if in_range(b):
-                quantise("x", side, b, side["passes"] * PIX, 3)
-
-        def project(side, b):
-            if not in_range(b):
+        def finish(s):
+            if not 0 <= s < len(steps):
                 return
-            passes = side["passes"]
-            x_codes = tiles["x_codes", side["name"], b]
-            x_scales = tiles["x_scales", side["name"], b]
-            for half in range(HALVES):
-                bank = banks.tile([P, BANK], F32, name="bank")
-                for t in range(PACK):
-                    for g in range(passes):
-                        w_cols = slice((t * passes + g) * P, (t * passes + g + 1) * P)
-                        x_cols = slice(g * PIX + half * P, g * PIX + (half + 1) * P)
-                        nc.tensor.matmul_mx(
-                            out=bank[:, t * P : (t + 1) * P],
-                            lhsT=side["w_codes"][:, w_cols].bitcast(FP8X4),
-                            lhsT_scale=side["w_scales"][:, w_cols],
-                            rhs=x_codes[:, x_cols].bitcast(FP8X4),
-                            rhs_scale=x_scales[:, x_cols],
-                            start=(g == 0),
-                            stop=(g == passes - 1),
-                        )
-                tiles["bank", side["name"], b, half] = bank
-
-        def add_bias(side, b):
-            if not in_range(b):
-                return
-            grouped = work.tile(
-                [P, PIX, PACK], BF16, name="y_grouped_" + side["name"], align_bytes=64
-            )
-            for half in range(HALVES):
-                nc.vector.tensor_tensor(
-                    out=grouped[:, half * P : (half + 1) * P, :],
-                    in0=tiles["bank", side["name"], b, half][:].rearrange(
-                        "p (t w) -> p w t", t=PACK
-                    ),
-                    in1=side["bias"][:].unsqueeze(1).to_broadcast([P, P, PACK]),
-                    op=ADD,
-                )
-            tiles["y_grouped", side["name"], b] = grouped
-
-        def quantise_y(side, b, bufs):
-            if in_range(b):
-                quantise("y", side, b, PIX, bufs)
-
-        def logits(b):
-            if not in_range(b):
-                return
-            logit = logit_banks.tile([P, HALVES, PIX], F32, name="logit")
-            for a in range(HALVES):
-                nc.tensor.matmul_mx(
-                    out=logit[:, a, :],
-                    lhsT=tiles["y_codes", "q", b][:, a * P : (a + 1) * P].bitcast(FP8X4),
-                    lhsT_scale=tiles["y_scales", "q", b][:, a * P : (a + 1) * P],
-                    rhs=tiles["y_codes", "k", b][:].bitcast(FP8X4),
-                    rhs_scale=tiles["y_scales", "k", b][:],
-                    start=True,
-                    stop=True,
-                )
-            tiles["logit", b] = logit
-
-        def store(b):
-            if not in_range(b):
-                return
-            result = work.tile([P, HALVES, PIX], F32, name="result", bufs=6)
-            nc.scalar.copy(out=result[:], in_=tiles["logit", b][:])
-            nc.sync.dma_start(out=out_dram[b], in_=result[:])
+            done = [b for (name, b) in steps[s] if name == "q"]
+            for b in done:
+                sq, slot_q = where["q", b]
+                sk, slot_k = where["k", b]
+                logit = logit_banks.tile([P, HALVES, PIX], F32, name="logit")
+                k_cols = slice(slot_k * PIX, (slot_k + 1) * PIX)
+                for a in range(HALVES):
+                    q_cols = slice(slot_q * PIX + a * P, slot_q * PIX + (a + 1) * P)
+                    nc.tensor.matmul_mx(
+                        out=logit[:, a, :],
+                        lhsT=tiles["y_codes", sq][:, q_cols].bitcast(FP8X4),
+                        lhsT_scale=tiles["y_scales", sq][:, q_cols],
+                        rhs=tiles["y_codes", sk][:, k_cols].bitcast(FP8X4),
+                        rhs_scale=tiles["y_scales", sk][:, k_cols],
+                        start=True,
+                        stop=True,
+                    )
+                tiles["logit", b] = logit
+            for b in done:
+                result = work.tile([P, HALVES, PIX], F32, name="result", bufs=4)
+                nc.scalar.copy(out=result[:], in_=tiles["logit", b][:])
+                nc.sync.dma_start(out=out_dram[b], in_=result[:])
 
         ident = const.tile([P, P], F32, name="ident")
         make_identity(nc, ident[:])
 
         load(k_side, 0)
         load_weight(k_side)
-        load(k_side, 1)
+        for b in range(1, 6):
+            load(k_side, b)
         load_weight(q_side)
-        load(k_side, 2)
+        for b in range(6, LEAD):
+            load(k_side, b)
         for b in range(IMAGES):
             load(q_side, b)
-            load(k_side, b + LEAD)
+            if b + LEAD < IMAGES:
+                load(k_side, b + LEAD)
 
-        regroup(k_side, 0)
-        quantise_x(k_side, 0)
+        def scalar_units(s):
+            return [u for u in units(s) if engine_of(u) == "scalar"]
+
+        regroup(("k", 0, 0))
+        quantise_x(("k", 0, 0))
         for t in range(PACK):
             transpose_weight(k_side, t)
             quantise_weight(k_side, t)
-        regroup(k_side, 1)
-        quantise_x(k_side, 1)
-        regroup(k_side, 2)
-        project(k_side, 0)
-        for t in range(PACK):
-            transpose_weight(q_side, t)
+        regroup(("k", 1, 0))
+        quantise_x(("k", 1, 0))
+        project(0)
+        for u in scalar_units(1) + scalar_units(2):
+            regroup(u)
+        transpose_weight(q_side, 0)
+        transpose_weight(q_side, 1)
 
-        for n in range(IMAGES + LEAD):
-            i = n - LEAD
-            add_bias(k_side, n)
-            project(k_side, n + 1)
-            add_bias(q_side, i)
-            if n == 1:
+        for s in range(len(steps)):
+            add_bias(s)
+            later = units(s + 2)
+            for u in later:
+                if engine_of(u) == "gpsimd":
+                    regroup(u)
+            finish(s - 1)
+            if s == 0:
+                for u in units(1):
+                    quantise_x(u)
+                project(1)
+                for u in scalar_units(3):
+                    regroup(u)
+                transpose_weight(q_side, 2)
+                transpose_weight(q_side, 3)
+                for r in range(4, 2 + AHEAD + 1):
+                    for u in scalar_units(r):
+                        regroup(u)
+            else:
+                project(s + 1)
+                for u in scalar_units(s + 2 + AHEAD):
+                    regroup(u)
+            for u in later:
+                if engine_of(u) != "gpsimd":
+                    quantise_x(u)
+            if s == LEAD // 2 - 2:
                 for t in range(PACK):
                     quantise_weight(q_side, t)
-            project(q_side, i + 1)
-            store(i - 1)
-            regroup(k_side, n + 3)
-            regroup(q_side, i + 3)
-            quantise_x(k_side, n + 2)
-            quantise_x(q_side, i + 2)
-            quantise_y(k_side, n, LEAD + 2)
-            quantise_y(q_side, i, 2)
-            logits(i)
-        store(IMAGES - 1)
+            quantise_y(s)
+            for u in later:
+                if engine_of(u) == "gpsimd":
+                    quantise_x(u)
+        finish(len(steps) - 1)

@@ -10,6 +10,7 @@ U8 = mybir.dt.uint8
 FP8X4 = mybir.dt.float8_e4m3fn_x4
 ADD = mybir.AluOpType.add
 MULT = mybir.AluOpType.mult
+IDENTITY = mybir.ActivationFunctionType.Identity
 
 P = 128
 PACK = 4
@@ -23,6 +24,7 @@ HID = 512
 
 LEAD = 8
 AHEAD = 3
+HELPED = 3
 
 FLOPS = 2 * IMAGES * PIX * (HID * 1024 + HID * 512 + PIX * HID)
 
@@ -191,26 +193,43 @@ def tile_crossattentionvaluefuser_pa_t_kernel(
 
         def add_bias(s):
             grouped = work.tile([P, 2, PIX, PACK], BF16, name="y_grouped", bufs=2, align_bytes=64)
+            tiles["y_grouped", s] = grouped
             for slot, (name, b) in enumerate(steps[s]):
                 for half in range(HALVES):
+                    bank = tiles["bank", name, b, half]
+                    if len(steps) - 1 - HELPED <= s < len(steps) - 1 and (slot, half) == (1, 1):
+                        for t in range(PACK):
+                            nc.scalar.activation(
+                                out=grouped[:, slot, half * P : (half + 1) * P, t],
+                                in_=bank[:, t * P : (t + 1) * P],
+                                func=IDENTITY,
+                                bias=sides[name]["bias"][:, t : t + 1],
+                                scale=1.0,
+                            )
+                        continue
                     nc.vector.tensor_tensor(
                         out=grouped[:, slot, half * P : (half + 1) * P, :],
-                        in0=tiles["bank", name, b, half][:].rearrange("p (t w) -> p w t", t=PACK),
+                        in0=bank[:].rearrange("p (t w) -> p w t", t=PACK),
                         in1=sides[name]["bias"][:].unsqueeze(1).to_broadcast([P, P, PACK]),
                         op=ADD,
                     )
-            tiles["y_grouped", s] = grouped
 
-        def quantise_y(s):
-            codes = work.tile([P, 2 * PIX], U32, name="y_codes", bufs=LEAD + 2, align_bytes=64)
-            scales = work.tile([P, 2 * PIX], U8, name="y_scales", bufs=LEAD + 2, align_bytes=64)
+        def quantise_y(s, slots):
+            if slots[0] == 0:
+                tiles["y_codes", s] = work.tile(
+                    [P, 2 * PIX], U32, name="y_codes", bufs=LEAD + 2, align_bytes=64
+                )
+                tiles["y_scales", s] = work.tile(
+                    [P, 2 * PIX], U8, name="y_scales", bufs=LEAD + 2, align_bytes=64
+                )
+            cols = slice(slots[0] * PIX, (slots[-1] + 1) * PIX)
             nc.vector.quantize_mx(
-                out=codes[:].bitcast(FP8X4),
-                scales=scales[:],
-                in_=tiles["y_grouped", s][:].rearrange("p a w t -> p (a w t)"),
+                out=tiles["y_codes", s][:, cols].bitcast(FP8X4),
+                scales=tiles["y_scales", s][:, cols],
+                in_=tiles["y_grouped", s][:, slots[0] : slots[-1] + 1, :, :].rearrange(
+                    "p a w t -> p (a w t)"
+                ),
             )
-            tiles["y_codes", s] = codes
-            tiles["y_scales", s] = scales
 
         def finish(s):
             if not 0 <= s < len(steps):
@@ -297,7 +316,11 @@ def tile_crossattentionvaluefuser_pa_t_kernel(
             if s == LEAD // 2 - 2:
                 for t in range(PACK):
                     quantise_weight(q_side, t)
-            quantise_y(s)
+            if s == len(steps) - 1:
+                quantise_y(s, [0])
+                quantise_y(s, [1])
+            else:
+                quantise_y(s, [0, 1])
             for u in later:
                 if engine_of(u) == "gpsimd":
                     quantise_x(u)

@@ -144,8 +144,8 @@ def tile_crossattentionvaluefuser_pa_t_kernel(
             raw = tiles["raw", name, b]
             if engine == "gpsimd":
                 nc.gpsimd.tensor_scalar(
-                    out=grouped[:].rearrange("p (w j) -> p w j", j=PACK),
-                    in0=raw[:, g, :].rearrange("p (j w) -> p w j", j=PACK),
+                    out=grouped[:].rearrange("p (c i j) -> p c j i", i=4, j=PACK),
+                    in0=raw[:, g, :].rearrange("p (j c i) -> p c j i", j=PACK, i=4),
                     scalar1=1.0,
                     scalar2=0.0,
                     op0=MULT,

from contextlib import ExitStack

import concourse.mybir as mybir
from concourse.masks import make_identity

F32 = mybir.dt.float32
BF16 = mybir.dt.bfloat16
U32 = mybir.dt.uint32
U8 = mybir.dt.uint8
FP8X4 = mybir.dt.float8_e4m3fn_x4
ADD = mybir.AluOpType.add
MULT = mybir.AluOpType.mult
IDENTITY = mybir.ActivationFunctionType.Identity

P = 128
PACK = 4
K_PASS = P * PACK
BANK = 512

IMAGES = 16
PIX = 256
HALVES = PIX // P
HID = 512

LEAD = 8
AHEAD = 3
HELPED = 3

FLOPS = 2 * IMAGES * PIX * (HID * 1024 + HID * 512 + PIX * HID)


def tile_crossattentionvaluefuser_pa_t_kernel(
    tc, query_features, reference_features, Wq, bq, Wk, bk, out
):
    nc = tc.nc
    sides = {
        "k": {"name": "k", "x": reference_features, "w": Wk, "b": bk},
        "q": {"name": "q", "x": query_features, "w": Wq, "b": bq},
    }
    k_side, q_side = sides["k"], sides["q"]
    for side in (k_side, q_side):
        side["passes"] = side["w"].shape[1] // K_PASS
    out_dram = out.rearrange("b (a i) j n -> b (i j) a n", a=HALVES)
    tiles = {}

    steps = [(("k", b), ("k", b + 1)) for b in range(0, LEAD, 2)]
    steps += [(("k", b + LEAD), ("q", b)) for b in range(IMAGES - LEAD)]
    steps += [(("q", b), ("q", b + 1)) for b in range(IMAGES - LEAD, IMAGES, 2)]
    where = {}
    for s, pair in enumerate(steps):
        for slot, job in enumerate(pair):
            where[job] = (s, slot)

    def units(s):
        if not 0 <= s < len(steps):
            return []
        return [(n, b, g) for (n, b) in steps[s] for g in range(sides[n]["passes"])]

    def engine_of(unit):
        s = where[unit[:2]][0]
        if s == 0:
            return "vector"
        if s >= 2 and unit == units(s)[-1]:
            return "gpsimd"
        return "scalar"

    with ExitStack() as ctx:
        const = ctx.enter_context(tc.tile_pool(name="const", bufs=1))
        inputs = ctx.enter_context(tc.tile_pool(name="inputs", bufs=IMAGES))
        work = ctx.enter_context(tc.tile_pool(name="work", bufs=2))
        banks = ctx.enter_context(tc.psum_pool(name="banks", bufs=6))
        logit_banks = ctx.enter_context(tc.psum_pool(name="logit_banks", bufs=2))
        ctx.enter_context(tc.manual_schedule())

        def load(side, b):
            raw = inputs.tile([P, side["passes"], PACK * PIX], BF16, name="raw_" + side["name"])
            nc.sync.dma_start(
                out=raw[:],
                in_=side["x"][b].rearrange("(g p j) h w -> p g (j h w)", p=P, j=PACK),
            )
            tiles["raw", side["name"], b] = raw

        def load_weight(side):
            cols = side["passes"] * K_PASS
            raw = const.tile([P, PACK * cols], BF16, name="w_raw_" + side["name"])
            rows = side["w"].rearrange("(m t) c -> m t c", t=PACK)
            for t in range(PACK):
                nc.sync.dma_start(out=raw[:, t * cols : (t + 1) * cols], in_=rows[:, t, :])
            side["w_raw"] = raw
            side["w_grouped"] = const.tile(
                [P, PACK * cols], BF16, name="w_grouped_" + side["name"], align_bytes=64
            )
            side["w_codes"] = const.tile(
                [P, cols], U32, name="w_codes_" + side["name"], align_bytes=64
            )
            side["w_scales"] = const.tile(
                [P, cols], U8, name="w_scales_" + side["name"], align_bytes=64
            )
            side["bias"] = const.tile([P, PACK], BF16, name="bias_" + side["name"])
            nc.scalar.dma_start(
                out=side["bias"][:], in_=side["b"].rearrange("(p t) -> p t", t=PACK)
            )

        def transpose_weight(side, t):
            passes = side["passes"]
            words = side["w_raw"][:].bitcast(F32).rearrange(
                "m (t g p u) -> m t g p u", t=PACK, g=passes, p=P, u=2
            )
            grouped_words = side["w_grouped"][:].bitcast(F32).rearrange(
                "p (t g m u) -> p t g m u", t=PACK, g=passes, m=P, u=2
            )
            if side["name"] == "k":
                bank = banks.tile([P, BANK], F32, name="bank")
            else:
                bank = logit_banks.tile([P, BANK], F32, name="logit")
            for g in range(passes):
                for u in range(2):
                    first = (g * 2 + u) * P
                    nc.tensor.transpose(bank[:, first : first + P], words[:, t, g, :, u], ident[:])
            nc.scalar.copy(
                out=grouped_words[:, t, :, :, :],
                in_=bank[:, : passes * 2 * P].rearrange("p (g u m) -> p g m u", g=passes, u=2),
            )

        def quantise_weight(side, t):
            width = side["passes"] * P
            nc.vector.quantize_mx(
                out=side["w_codes"][:, t * width : (t + 1) * width].bitcast(FP8X4),
                scales=side["w_scales"][:, t * width : (t + 1) * width],
                in_=side["w_grouped"][:, t * PACK * width : (t + 1) * PACK * width],
            )

        def regroup(unit):
            name, b, g = unit
            engine = engine_of(unit)
            if engine == "scalar":
                grouped = work.tile(
                    [P, PACK * PIX], BF16, name="x_grouped", bufs=4 * (AHEAD + 1), align_bytes=64
                )
            else:
                grouped = work.tile(
                    [P, PACK * PIX], BF16, name="x_grouped_port", bufs=1, align_bytes=64
                )
            raw = tiles["raw", name, b]
            if engine == "gpsimd":
                nc.gpsimd.tensor_scalar(
                    out=grouped[:].rearrange("p (c i j) -> p c j i", i=4, j=PACK),
                    in0=raw[:, g, :].rearrange("p (j c i) -> p c j i", j=PACK, i=4),
                    scalar1=1.0,
                    scalar2=0.0,
                    op0=MULT,
                    op1=ADD,
                )
            else:
                copy = nc.vector.tensor_copy if engine == "vector" else nc.scalar.copy
                copy(
                    out=grouped[:].rearrange("p (c i j) -> p c j i", i=4, j=PACK),
                    in_=raw[:, g, :].rearrange("p (j c i) -> p c j i", j=PACK, i=4),
                )
            tiles["x_grouped", unit] = grouped

        def quantise_x(unit):
            codes = work.tile([P, PIX], U32, name="x_codes", bufs=10, align_bytes=64)
            scales = work.tile([P, PIX], U8, name="x_scales", bufs=10, align_bytes=64)
            nc.vector.quantize_mx(
                out=codes[:].bitcast(FP8X4), scales=scales[:], in_=tiles["x_grouped", unit][:]
            )
            tiles["x_codes", unit] = codes
            tiles["x_scales", unit] = scales

        def project(s):
            if not 0 <= s < len(steps):
                return
            for name, b in steps[s]:
                side = sides[name]
                passes = side["passes"]
                for half in range(HALVES):
                    bank = banks.tile([P, BANK], F32, name="bank")
                    for t in range(PACK):
                        for g in range(passes):
                            w_cols = slice((t * passes + g) * P, (t * passes + g + 1) * P)
                            x_cols = slice(half * P, (half + 1) * P)
                            nc.tensor.matmul_mx(
                                out=bank[:, t * P : (t + 1) * P],
                                lhsT=side["w_codes"][:, w_cols].bitcast(FP8X4),
                                lhsT_scale=side["w_scales"][:, w_cols],
                                rhs=tiles["x_codes", (name, b, g)][:, x_cols].bitcast(FP8X4),
                                rhs_scale=tiles["x_scales", (name, b, g)][:, x_cols],
                                start=(g == 0),
                                stop=(g == passes - 1),
                            )
                    tiles["bank", name, b, half] = bank

        def add_bias(s):
            grouped = work.tile([P, 2, PIX, PACK], BF16, name="y_grouped", bufs=2, align_bytes=64)
            tiles["y_grouped", s] = grouped
            for slot, (name, b) in enumerate(steps[s]):
                for half in range(HALVES):
                    bank = tiles["bank", name, b, half]
                    if len(steps) - 1 - HELPED <= s < len(steps) - 1 and (slot, half) == (1, 1):
                        for t in range(PACK):
                            nc.scalar.activation(
                                out=grouped[:, slot, half * P : (half + 1) * P, t],
                                in_=bank[:, t * P : (t + 1) * P],
                                func=IDENTITY,
                                bias=sides[name]["bias"][:, t : t + 1],
                                scale=1.0,
                            )
                        continue
                    nc.vector.tensor_tensor(
                        out=grouped[:, slot, half * P : (half + 1) * P, :],
                        in0=bank[:].rearrange("p (t w) -> p w t", t=PACK),
                        in1=sides[name]["bias"][:].unsqueeze(1).to_broadcast([P, P, PACK]),
                        op=ADD,
                    )

        def quantise_y(s, slots):
            if slots[0] == 0:
                tiles["y_codes", s] = work.tile(
                    [P, 2 * PIX], U32, name="y_codes", bufs=LEAD + 2, align_bytes=64
                )
                tiles["y_scales", s] = work.tile(
                    [P, 2 * PIX], U8, name="y_scales", bufs=LEAD + 2, align_bytes=64
                )
            cols = slice(slots[0] * PIX, (slots[-1] + 1) * PIX)
            nc.vector.quantize_mx(
                out=tiles["y_codes", s][:, cols].bitcast(FP8X4),
                scales=tiles["y_scales", s][:, cols],
                in_=tiles["y_grouped", s][:, slots[0] : slots[-1] + 1, :, :].rearrange(
                    "p a w t -> p (a w t)"
                ),
            )

        def finish(s):
            if not 0 <= s < len(steps):
                return
            done = [b for (name, b) in steps[s] if name == "q"]
            for b in done:
                sq, slot_q = where["q", b]
                sk, slot_k = where["k", b]
                logit = logit_banks.tile([P, HALVES, PIX], F32, name="logit")
                k_cols = slice(slot_k * PIX, (slot_k + 1) * PIX)
                for a in range(HALVES):
                    q_cols = slice(slot_q * PIX + a * P, slot_q * PIX + (a + 1) * P)
                    nc.tensor.matmul_mx(
                        out=logit[:, a, :],
                        lhsT=tiles["y_codes", sq][:, q_cols].bitcast(FP8X4),
                        lhsT_scale=tiles["y_scales", sq][:, q_cols],
                        rhs=tiles["y_codes", sk][:, k_cols].bitcast(FP8X4),
                        rhs_scale=tiles["y_scales", sk][:, k_cols],
                        start=True,
                        stop=True,
                    )
                tiles["logit", b] = logit
            for b in done:
                result = work.tile([P, HALVES, PIX], F32, name="result", bufs=4)
                nc.scalar.copy(out=result[:], in_=tiles["logit", b][:])
                nc.sync.dma_start(out=out_dram[b], in_=result[:])

        ident = const.tile([P, P], F32, name="ident")
        make_identity(nc, ident[:])

        load(k_side, 0)
        load_weight(k_side)
        for b in range(1, 6):
            load(k_side, b)
        load_weight(q_side)
        for b in range(6, LEAD):
            load(k_side, b)
        for b in range(IMAGES):
            load(q_side, b)
            if b + LEAD < IMAGES:
                load(k_side, b + LEAD)

        def scalar_units(s):
            return [u for u in units(s) if engine_of(u) == "scalar"]

        regroup(("k", 0, 0))
        quantise_x(("k", 0, 0))
        for t in range(PACK):
            transpose_weight(k_side, t)
            quantise_weight(k_side, t)
        regroup(("k", 1, 0))
        quantise_x(("k", 1, 0))
        project(0)
        for u in scalar_units(1) + scalar_units(2):
            regroup(u)
        transpose_weight(q_side, 0)
        transpose_weight(q_side, 1)

        for s in range(len(steps)):
            add_bias(s)
            later = units(s + 2)
            for u in later:
                if engine_of(u) == "gpsimd":
                    regroup(u)
            finish(s - 1)
            if s == 0:
                for u in units(1):
                    quantise_x(u)
                project(1)
                for u in scalar_units(3):
                    regroup(u)
                transpose_weight(q_side, 2)
                transpose_weight(q_side, 3)
                for r in range(4, 2 + AHEAD + 1):
                    for u in scalar_units(r):
                        regroup(u)
            else:
                project(s + 1)
                for u in scalar_units(s + 2 + AHEAD):
                    regroup(u)
            for u in later:
                if engine_of(u) != "gpsimd":
                    quantise_x(u)
            if s == LEAD // 2 - 2:
                for t in range(PACK):
                    quantise_weight(q_side, t)
            if s == len(steps) - 1:
                quantise_y(s, [0])
                quantise_y(s, [1])
            else:
                quantise_y(s, [0, 1])
            for u in later:
                if engine_of(u) == "gpsimd":
                    quantise_x(u)
        finish(len(steps) - 1)
